import numpy as np
import ml_dtypes


def mxq(x, axis, fmt="e4m3"):
    dtype, down = {"e4m3": (ml_dtypes.float8_e4m3fn, 7), "e5m2": (ml_dtypes.float8_e5m2, 14)}[fmt]
    v = np.moveaxis(np.asarray(x, np.float32).astype(ml_dtypes.bfloat16).astype(np.float64), axis, -1)
    blocks = v.reshape(v.shape[:-1] + (-1, 32))
    amax = np.abs(blocks).max(-1, keepdims=True)
    byte = np.maximum(np.where(amax > 0, np.frexp(amax)[1] - 1 + 127, 0) - down, 1)
    scale = np.exp2(byte - 127.0)
    codes = (blocks / scale).astype(np.float32).astype(dtype).astype(np.float64)
    return np.moveaxis((codes * scale).reshape(v.shape), -1, axis)


WIDE = False


def mx_kscale(k):
    if not WIDE:
        return np.ones(k)
    levels = np.array([10, -10, 5, -5, 0])
    if k % 512:
        return np.exp2(np.random.permutation(np.resize(levels, k // 32))).repeat(32)
    a = np.empty((k // 512, 16))
    for p in range(k // 512):
        a[p, :8] = np.random.permutation(np.resize(levels, 8))
        for g in range(8):
            far = levels[np.abs(levels - a[p, g]) >= 10]
            a[p, g + 8] = far[np.random.randint(len(far))]
    return np.exp2(a.ravel()).repeat(32)


BF16 = ml_dtypes.bfloat16


def bf(x):
    return np.asarray(x, np.float32).astype(BF16)


def f64(x):
    return np.asarray(x).astype(np.float64)


B, G0, G1, C0, C1, NC = 8, 8, 4, 512, 512, 250
NCH = 5 + 1 + NC
STRIDES = [8, 16]
SXY = [1.2, 1.1]
ANCH = [[[10, 13], [16, 30], [33, 23]], [[30, 61], [62, 45], [59, 119]]]
RAD = np.pi / 180.0
ANGLES = [RAD * a for a in (-60.0, -30.0, 0.0, 30.0, 60.0, 90.0)]
NA = len(ANCH[0]) * len(ANGLES)
O = NA * NCH
T = B * G0 * G0
N0 = NA * G0 * G0
N1 = NA * G1 * G1


def sigmoid(v):
    return 1.0 / (1.0 + np.exp(-v))


def _masked_anchors(level):
    s = STRIDES[level]
    return np.array([[w / s, h / s, a] for (w, h) in ANCH[level] for a in ANGLES], dtype=np.float64)


def _preact(feat, W, b):
    Bn, C, G, _ = feat.shape
    p = W @ feat.reshape(Bn, C, G * G) + b[None, :, None]
    return p.reshape(Bn, NA, NCH, G * G).transpose(0, 1, 3, 2).reshape(Bn, NA * G * G, NCH)


def _dfield(z, level):
    s = float(STRIDES[level])
    ma = _masked_anchors(level)
    sg = sigmoid(z)
    d = sg * (1.0 - sg)
    d[..., 0:2] = d[..., 0:2] * (SXY[level] * s)
    d[..., 2] = np.exp(z[..., 2]) * (ma[:, 0] * s)[None, :, None]
    d[..., 3] = np.exp(z[..., 3]) * (ma[:, 1] * s)[None, :, None]
    d[..., 4] = 1.0
    return d


def _draw_level(G, C):
    g = np.full(NCH, 1.5)
    g[2:4] = 0.3
    x = np.random.standard_normal((B, C, G, G))
    W = np.random.standard_normal((NA, NCH, C)) * g[None, :, None] / np.sqrt(C)
    b = np.random.standard_normal((NA, NCH)) * 0.4
    b[:, 2:4] -= 2.0
    return bf(x), bf(W.reshape(NA * NCH, C)), bf(b.reshape(NA * NCH))


def setup_inputs():
    s = mx_kscale(T).reshape(B, G0, G0)
    u = mx_kscale(O)
    x00, W00, b0 = _draw_level(G0, C0)
    x1, W1, b1 = _draw_level(G1, C1)
    g = np.random.standard_normal((B, N0 + N1, NCH)) * np.exp2(np.random.randint(-6, 1, (B, N0 + N1, 1))) * 4.0
    g[:, :N0] = (g[:, :N0].reshape(B, NA, G0 * G0, NCH) / s.reshape(B, 1, G0 * G0, 1)
                 * u.reshape(1, NA, 1, NCH)).reshape(B, N0, NCH)
    z0 = _preact(f64(x00), f64(W00), f64(b0))
    x0 = bf(f64(x00) * s[:, None, :, :])
    W0 = bf(f64(W00) / u[:, None])
    return {"x0": x0, "x1": x1, "W0": W0, "b0": b0, "W1": W1, "b1": b1,
            "z0": np.asarray(z0, np.float32), "grad_out": bf(g)}


def reference(x0, x1, W0, b0, W1, b1, z0, grad_out):
    z = f64(z0).reshape(B, NA, G0 * G0, NCH)
    g = f64(grad_out)[:, :N0].reshape(B, NA, G0 * G0, NCH)
    dz = g * _dfield(z, 0)
    dz = dz.transpose(0, 2, 1, 3).reshape(T, O)
    x = f64(x0).reshape(B, C0, G0 * G0).transpose(0, 2, 1).reshape(T, C0)
    dx = mxq(dz, 1, "e5m2") @ mxq(f64(W0), 0, "e4m3")
    dw = mxq(dz, 0, "e5m2").T @ mxq(x, 0, "e4m3")
    dx0 = np.ascontiguousarray(dx.reshape(B, G0, G0, C0).transpose(0, 3, 1, 2))
    return dx0, dw

@@ -1,0 +1,313 @@
+from contextlib import ExitStack
+
+import concourse.mybir as mybir
+from concourse.masks import make_identity
+
+F32 = mybir.dt.float32
+BF16 = mybir.dt.bfloat16
+U32 = mybir.dt.uint32
+U8 = mybir.dt.uint8
+E4X4 = mybir.dt.float8_e4m3fn_x4
+E5X4 = mybir.dt.float8_e5m2_x4
+ALU = mybir.AluOpType
+ACT = mybir.ActivationFunctionType
+
+P = 128
+NB = 8
+NCH = 9
+C = 512
+SHAPES = ((10.0, 13.0), (16.0, 30.0), (33.0, 23.0))
+B_ORDER = (0, 1, 4, 5, 2, 3, 6, 7)
+
+FLOPS = 2 * 2 * 512 * 4608 * 512
+BYTES = 524288 + 4718592 + 9437184 + 4718592 + 1048576 + 9437184
+
+
+def tile_detect_v_kernel(tc, x0, x1, W0, b0, W1, b1, z0, grad_out, out_0, out_1):
+    nc = tc.nc
+    with ExitStack() as ctx:
+        const = ctx.enter_context(tc.tile_pool(name="const", bufs=1))
+        zpool = ctx.enter_context(tc.tile_pool(name="zpool", bufs=4))
+        gpool = ctx.enter_context(tc.tile_pool(name="gpool", bufs=4))
+        wpool = ctx.enter_context(tc.tile_pool(name="wpool", bufs=3))
+        work = ctx.enter_context(tc.tile_pool(name="work", bufs=2))
+        codes = ctx.enter_context(tc.tile_pool(name="codes", bufs=3))
+        stage = ctx.enter_context(tc.tile_pool(name="stage", bufs=6))
+        accp = ctx.enter_context(tc.psum_pool(name="accp", bufs=1))
+        tpp = ctx.enter_context(tc.psum_pool(name="tpp", bufs=2))
+        o1p = ctx.enter_context(tc.psum_pool(name="o1p", bufs=2))
+        ctx.enter_context(tc.manual_schedule())
+
+        zs = {}
+        gs = {}
+        ws = {}
+        exs = {}
+        wgs = {}
+        wcs = {}
+        dns = {}
+        tps = {}
+        ggs = {}
+        gcs = {}
+        ais = {}
+        acs = {}
+        o1s = {}
+        sts = {}
+
+        def ok(ch):
+            return 0 <= ch < NCH
+
+        def load(ch):
+            if not ok(ch):
+                return
+            zt = zpool.tile([P, 2, 4, 256], F32, name="zt")
+            gt = gpool.tile([P, 2, 4, 256], BF16, name="gt")
+            for b in B_ORDER:
+                nc.sync.dma_start(
+                    out=zt[16 * b : 16 * b + 16],
+                    in_=z0[b, 128 * ch : 128 * ch + 128, :].rearrange("(a q j) f -> q a j f", a=2, q=16, j=4),
+                )
+            for b in B_ORDER:
+                nc.sync.dma_start(
+                    out=gt[16 * b : 16 * b + 16],
+                    in_=grad_out[b, 128 * ch : 128 * ch + 128, :].rearrange("(a q j) f -> q a j f", a=2, q=16, j=4),
+                )
+            zs[ch] = zt
+            gs[ch] = gt
+
+        def load_w(ch):
+            if not ok(ch):
+                return
+            wraw = wpool.tile([P, 4, C], BF16, name="wraw")
+            nc.sync.dma_start(out=wraw[:], in_=W0[512 * ch : 512 * ch + 512, :].rearrange("(p t) c -> p t c", t=4))
+            ws[ch] = wraw
+
+        def act_e(ch):
+            if not ok(ch):
+                return
+            zt = zs[ch]
+            ex = work.tile([P, 2, 4, 2], F32, name="ex")
+            nc.scalar.activation(out=ex[:], in_=zt[:, :, :, 2:4], func=ACT.Exp)
+            zf = zt[:].rearrange("p a j f -> p (a j f)")
+            nc.scalar.activation(out=zf, in_=zf, func=ACT.Tanh, scale=0.5)
+            nc.scalar.activation(out=zf, in_=zf, func=ACT.Square, scale=0.5)
+            exs[ch] = ex
+
+        def patches(ch):
+            if not ok(ch):
+                return
+            zt = zs[ch]
+            nc.vector.tensor_scalar(out=zt[:, :, :, 0:2], in0=zt[:, :, :, 0:2], scalar1=9.6, scalar2=-2.15,
+                                    op0=ALU.mult, op1=ALU.add)
+            nc.vector.memset(zt[:, :, :, 4:5], -0.75)
+
+        def w_int(ch):
+            if not ok(ch):
+                return
+            wg = work.tile([P, C, 4], BF16, name="wg", align_bytes=64)
+            nc.vector.tensor_copy(out=wg[:], in_=ws.pop(ch)[:].rearrange("p t c -> p c t"))
+            wgs[ch] = wg
+
+        def w_quant(ch):
+            if not ok(ch):
+                return
+            wc = codes.tile([P, C], U32, name="wc", align_bytes=64)
+            wsc = codes.tile([P, C], U8, name="wsc", align_bytes=64)
+            nc.vector.quantize_mx(out=wc[:].bitcast(E4X4), scales=wsc[:], in_=wgs.pop(ch)[:].rearrange("p c t -> p (c t)"))
+            wcs[ch] = (wc, wsc)
+
+        def p3(ch):
+            if not ok(ch):
+                return
+            dn = work.tile([P, 4, 2, 256], BF16, name="dn", align_bytes=64)
+            for a in range(2):
+                nc.vector.scalar_tensor_tensor(out=dn[:, :, a, :], in0=zs[ch][:, a], scalar=0.25, in1=gs[ch][:, a],
+                                               op0=ALU.subtract, op1=ALU.mult)
+            dns[ch] = dn
+
+        def spec(ch):
+            if not ok(ch):
+                return
+            wsh, hsh = SHAPES[ch // 3]
+            ex = exs.pop(ch)
+            gt = gs.pop(ch)
+            zs.pop(ch)
+            dnv = dns[ch][:].rearrange("p j a f -> p a j f")
+            nc.vector.scalar_tensor_tensor(out=dnv[:, :, :, 2:3], in0=ex[:, :, :, 0:1], scalar=-wsh,
+                                           in1=gt[:, :, :, 2:3], op0=ALU.mult, op1=ALU.mult)
+            nc.vector.scalar_tensor_tensor(out=dnv[:, :, :, 3:4], in0=ex[:, :, :, 1:2], scalar=-hsh,
+                                           in1=gt[:, :, :, 3:4], op0=ALU.mult, op1=ALU.mult)
+
+        def t1(ch):
+            if not ok(ch):
+                return
+            dw = dns[ch][:].rearrange("p j a f -> p (j a f)").bitcast(F32)
+            pair = []
+            for h in range(2):
+                tp = tpp.tile([P, 2, 2, P], F32, name="tp")
+                for k in range(2):
+                    j = 2 * h + k
+                    for u in range(2):
+                        nc.tensor.transpose(tp[:, k, u, :], dw[:, 256 * j + u : 256 * (j + 1) : 2], ident[:])
+                pair.append(tp)
+            tps[ch] = pair
+
+        def a_int(ch):
+            if not ok(ch):
+                return
+            ai = work.tile([P, 512, 4], BF16, name="ai", align_bytes=64)
+            nc.vector.tensor_copy(out=ai[:], in_=dns.pop(ch)[:].rearrange("p j a f -> p (a f) j"))
+            ais[ch] = ai
+
+        def tp_out(ch):
+            if not ok(ch):
+                return
+            gg = work.tile([P, 4, P, 4], BF16, name="gg", align_bytes=64)
+            ggw = gg[:].rearrange("p j r t -> p (j r t)").bitcast(F32).rearrange("p (j r u) -> p j r u", j=4, r=128, u=2)
+            pair = tps.pop(ch)
+            nc.scalar.copy(out=ggw[:, 0:2], in_=pair[0][:].rearrange("p k u r -> p k r u"))
+            nc.vector.tensor_copy(out=ggw[:, 2:4], in_=pair[1][:].rearrange("p k u r -> p k r u"))
+            ggs[ch] = gg
+
+        def a_quant(ch):
+            if not ok(ch):
+                return
+            ac = codes.tile([P, 512], U32, name="ac", align_bytes=64)
+            asc = codes.tile([P, 512], U8, name="asc", align_bytes=64)
+            nc.vector.quantize_mx(out=ac[:].bitcast(E5X4), scales=asc[:], in_=ais.pop(ch)[:].rearrange("p o j -> p (o j)"))
+            acs[ch] = (ac, asc)
+
+        def g_quant(ch):
+            if not ok(ch):
+                return
+            gc = codes.tile([P, 512], U32, name="gc", align_bytes=64)
+            gsc = codes.tile([P, 512], U8, name="gsc", align_bytes=64)
+            nc.vector.quantize_mx(out=gc[:].bitcast(E5X4), scales=gsc[:], in_=ggs.pop(ch)[:].rearrange("p j r t -> p (j r t)"))
+            gcs[ch] = (gc, gsc)
+
+        def mm1(ch, m):
+            if not ok(ch):
+                return
+            ac, asc = acs[ch]
+            o1 = o1p.tile([P, C], F32, name="o1")
+            nc.tensor.matmul_mx(out=o1[:], lhsT=ac[:, 128 * m : 128 * m + 128].bitcast(E5X4),
+                                lhsT_scale=asc[:, 128 * m : 128 * m + 128],
+                                rhs=xc[:].bitcast(E4X4), rhs_scale=xs[:], start=True, stop=True)
+            o1s[(ch, m)] = o1
+
+        def evict(ch, m, on_vector):
+            if not ok(ch):
+                return
+            if m % 2 == 0:
+                st = stage.tile([P, 2, C], F32, name="st")
+                sts[(ch, m // 2)] = st
+            st = sts[(ch, m // 2)]
+            o1 = o1s.pop((ch, m))
+            if on_vector:
+                nc.vector.tensor_scalar(out=st[:, m % 2, :], in0=o1[:], scalar1=-1.0, scalar2=None, op0=ALU.mult)
+            else:
+                nc.scalar.activation(out=st[:, m % 2, :], in_=o1[:], func=ACT.Copy, scale=-1.0)
+
+        def store(ch, half):
+            if not ok(ch):
+                return
+            r0 = 512 * ch + 256 * half
+            nc.sync.dma_start(out=out_1[r0 : r0 + 256, :].rearrange("(m p) c -> p m c", m=2), in_=sts.pop((ch, half))[:])
+
+        def mm0(ch):
+            if not ok(ch):
+                return
+            wc, wsc = wcs.pop(ch)
+            gc, gsc = gcs.pop(ch)
+            for ct in range(4):
+                nc.tensor.matmul_mx(out=acc[ct][:], lhsT=wc[:, 128 * ct : 128 * ct + 128].bitcast(E4X4),
+                                    lhsT_scale=wsc[:, 128 * ct : 128 * ct + 128],
+                                    rhs=gc[:].bitcast(E5X4), rhs_scale=gsc[:],
+                                    start=(ch == 0), stop=(ch == NCH - 1))
+
+        def evict0(ct, on_vector):
+            o0 = stage.tile([P, P, 4], F32, name="o0")
+            src = acc[ct][:].rearrange("c (j r) -> c r j", j=4)
+            if on_vector:
+                nc.vector.tensor_scalar(out=o0[:], in0=src, scalar1=-1.0, scalar2=None, op0=ALU.mult)
+            else:
+                nc.scalar.activation(out=o0[:], in_=src, func=ACT.Copy, scale=-1.0)
+            nc.sync.dma_start(
+                out=out_0[:, 128 * ct : 128 * ct + 128, :, :].rearrange("b c gy gx -> c b (gy gx)"),
+                in_=o0[:].rearrange("c r j -> c (r j)").rearrange("c (b s) -> c b s", b=NB),
+            )
+
+        warm = const.tile([P, 1], F32, name="warm")
+        nc.vector.memset(warm[:], 0.0)
+        warm2 = const.tile([P, 1], F32, name="warm2")
+        nc.scalar.activation(out=warm2[:], in_=warm[:], func=ACT.Exp)
+        ident = const.tile([P, P], F32, name="ident")
+        make_identity(nc, ident[:])
+        acc = [accp.tile([P, 512], F32, name="acc%d" % ct) for ct in range(4)]
+
+        load(0)
+        load_w(0)
+        xraw = const.tile([P, 4, 512], BF16, name="xraw")
+        for cb in range(4):
+            nc.sync.dma_start(
+                out=xraw[:, cb, :].rearrange("c (b s) -> c b s", b=NB),
+                in_=x0[:, 128 * cb : 128 * cb + 128, :, :].rearrange("b c gy gx -> c b (gy gx)"),
+            )
+        load_w(1)
+        load(1)
+        load_w(2)
+        load(2)
+
+        act_e(0)
+        w_int(0)
+        xw = xraw[:].rearrange("c cb t -> c (cb t)").bitcast(F32)
+        xg = const.tile([P, C, 4], BF16, name="xg", align_bytes=64)
+        xgw = xg[:].rearrange("p c t -> p (c t)").bitcast(F32).rearrange("p (cb c u) -> p cb c u", cb=4, c=128, u=2)
+        for h in range(2):
+            tp = tpp.tile([P, 2, 2, P], F32, name="tp")
+            for k in range(2):
+                cb = 2 * h + k
+                for u in range(2):
+                    nc.tensor.transpose(tp[:, k, u, :], xw[:, 256 * cb + u : 256 * (cb + 1) : 2], ident[:])
+            nc.vector.tensor_copy(out=xgw[:, 2 * h : 2 * h + 2], in_=tp[:].rearrange("p k u r -> p k r u"))
+        w_quant(0)
+        xc = const.tile([P, C], U32, name="xc", align_bytes=64)
+        xs = const.tile([P, C], U8, name="xs", align_bytes=64)
+        nc.vector.quantize_mx(out=xc[:].bitcast(E4X4), scales=xs[:], in_=xg[:].rearrange("p c t -> p (c t)"))
+        patches(0)
+
+        for k in range(0, NCH + 1):
+            last = k - 1 == NCH - 1
+            store(k - 2, 0)
+            store(k - 2, 1)
+            load_w(k + 3)
+            load(k + 3)
+            act_e(k + 1)
+            p3(k)
+            if k == 0:
+                w_int(1)
+            w_quant(k + 1)
+            spec(k)
+            t1(k)
+            w_int(k + 2)
+            a_int(k)
+            tp_out(k)
+            a_quant(k)
+            evict(k - 1, 0, False)
+            mm1(k - 1, 2)
+            evict(k - 1, 1, last)
+            mm1(k - 1, 3)
+            if last:
+                store(k - 1, 0)
+                evict0(0, False)
+                evict0(1, True)
+            evict(k - 1, 2, False)
+            evict(k - 1, 3, last)
+            if last:
+                store(k - 1, 1)
+                evict0(2, False)
+                evict0(3, True)
+            patches(k + 1)
+            g_quant(k)
+            mm1(k, 0)
+            mm1(k, 1)
+            mm0(k)

@@ -62,12 +62,14 @@ def tile_detect_v_kernel(tc, x0, x1, W0, b0, W1, b1, z0, grad_out, out_0, out_1)
             zt = zpool.tile([P, 2, 4, 256], F32, name="zt")
             gt = gpool.tile([P, 2, 4, 256], BF16, name="gt")
             for b in B_ORDER:
-                nc.sync.dma_start(
+                ring = nc.sync if b % 2 == 0 else nc.gpsimd
+                ring.dma_start(
                     out=zt[16 * b : 16 * b + 16],
                     in_=z0[b, 128 * ch : 128 * ch + 128, :].rearrange("(a q j) f -> q a j f", a=2, q=16, j=4),
                 )
             for b in B_ORDER:
-                nc.sync.dma_start(
+                ring = nc.sync if b % 2 == 0 else nc.gpsimd
+                ring.dma_start(
                     out=gt[16 * b : 16 * b + 16],
                     in_=grad_out[b, 128 * ch : 128 * ch + 128, :].rearrange("(a q j) f -> q a j f", a=2, q=16, j=4),
                 )

@@ -23,6 +23,9 @@ FLOPS = 2 * 2 * 512 * 4608 * 512
 BYTES = 524288 + 4718592 + 9437184 + 4718592 + 1048576 + 9437184
 
 
+IMG_ORDER = (0, 2, 1, 3, 4, 6, 5, 7)
+
+
 def tile_detect_v_kernel(tc, x0, x1, W0, b0, W1, b1, z0, grad_out, out_0, out_1):
     nc = tc.nc
     with ExitStack() as ctx:
@@ -32,14 +35,15 @@ def tile_detect_v_kernel(tc, x0, x1, W0, b0, W1, b1, z0, grad_out, out_0, out_1)
         wpool = ctx.enter_context(tc.tile_pool(name="wpool", bufs=3))
         work = ctx.enter_context(tc.tile_pool(name="work", bufs=2))
         codes = ctx.enter_context(tc.tile_pool(name="codes", bufs=3))
-        stage = ctx.enter_context(tc.tile_pool(name="stage", bufs=6))
+        stage = ctx.enter_context(tc.tile_pool(name="stage", bufs=18))
+        stage0 = ctx.enter_context(tc.tile_pool(name="stage0", bufs=4))
         accp = ctx.enter_context(tc.psum_pool(name="accp", bufs=1))
         tpp = ctx.enter_context(tc.psum_pool(name="tpp", bufs=2))
         o1p = ctx.enter_context(tc.psum_pool(name="o1p", bufs=2))
         ctx.enter_context(tc.manual_schedule())
 
-        zs = {}
-        gs = {}
+        zg = {}
+        gg_in = {}
         ws = {}
         exs = {}
         wgs = {}
@@ -48,6 +52,7 @@ def tile_detect_v_kernel(tc, x0, x1, W0, b0, W1, b1, z0, grad_out, out_0, out_1)
         tps = {}
         ggs = {}
         gcs = {}
+        tys = {}
         ais = {}
         acs = {}
         o1s = {}
@@ -59,22 +64,25 @@ def tile_detect_v_kernel(tc, x0, x1, W0, b0, W1, b1, z0, grad_out, out_0, out_1)
         def load(ch):
             if not ok(ch):
                 return
-            zt = zpool.tile([P, 2, 4, 256], F32, name="zt")
-            gt = gpool.tile([P, 2, 4, 256], BF16, name="gt")
-            for b in B_ORDER:
-                ring = nc.sync if b % 2 == 0 else nc.gpsimd
-                ring.dma_start(
-                    out=zt[16 * b : 16 * b + 16],
-                    in_=z0[b, 128 * ch : 128 * ch + 128, :].rearrange("(a q j) f -> q a j f", a=2, q=16, j=4),
+            zt = zpool.tile([P, 2, 2, 2, 256], F32, name="zt")
+            gt = gpool.tile([P, 2, 2, 2, 256], BF16, name="gt")
+            for b in IMG_ORDER:
+                lo = 32 * (b % 4)
+                nc.sync.dma_start(
+                    out=zt[lo : lo + 32, b // 4],
+                    in_=z0[b, 128 * ch : 128 * ch + 128, :].rearrange("(a q j) f -> q a j f", a=2, q=32, j=2),
                 )
-            for b in B_ORDER:
-                ring = nc.sync if b % 2 == 0 else nc.gpsimd
-                ring.dma_start(
-                    out=gt[16 * b : 16 * b + 16],
-                    in_=grad_out[b, 128 * ch : 128 * ch + 128, :].rearrange("(a q j) f -> q a j f", a=2, q=16, j=4),
+            for b in IMG_ORDER:
+                lo = 32 * (b % 4)
+                nc.sync.dma_start(
+                    out=gt[lo : lo + 32, b // 4],
+                    in_=grad_out[b, 128 * ch : 128 * ch + 128, :].rearrange("(a q j) f -> q a j f", a=2, q=32, j=2),
                 )
-            zs[ch] = zt
-            gs[ch] = gt
+            zg[ch] = zt
+            gg_in[ch] = gt
+
+        def zc_of(ch):
+            return zg[ch][:], gg_in[ch][:]
 
         def load_w(ch):
             if not ok(ch):
@@ -86,10 +94,10 @@ def tile_detect_v_kernel(tc, x0, x1, W0, b0, W1, b1, z0, grad_out, out_0, out_1)
         def act_e(ch):
             if not ok(ch):
                 return
-            zt = zs[ch]
-            ex = work.tile([P, 2, 4, 2], F32, name="ex")
-            nc.scalar.activation(out=ex[:], in_=zt[:, :, :, 2:4], func=ACT.Exp)
-            zf = zt[:].rearrange("p a j f -> p (a j f)")
+            zc, gc_in = zc_of(ch)
+            ex = work.tile([P, 2, 2, 2, 2], F32, name="ex")
+            nc.scalar.activation(out=ex[:], in_=zc[:, :, :, :, 2:4], func=ACT.Exp)
+            zf = zc.rearrange("p g a j f -> p g (a j f)")
             nc.scalar.activation(out=zf, in_=zf, func=ACT.Tanh, scale=0.5)
             nc.scalar.activation(out=zf, in_=zf, func=ACT.Square, scale=0.5)
             exs[ch] = ex
@@ -97,10 +105,10 @@ def tile_detect_v_kernel(tc, x0, x1, W0, b0, W1, b1, z0, grad_out, out_0, out_1)
         def patches(ch):
             if not ok(ch):
                 return
-            zt = zs[ch]
-            nc.vector.tensor_scalar(out=zt[:, :, :, 0:2], in0=zt[:, :, :, 0:2], scalar1=9.6, scalar2=-2.15,
+            zc, gc_in = zc_of(ch)
+            nc.vector.tensor_scalar(out=zc[:, :, :, :, 0:2], in0=zc[:, :, :, :, 0:2], scalar1=9.6, scalar2=-2.15,
                                     op0=ALU.mult, op1=ALU.add)
-            nc.vector.memset(zt[:, :, :, 4:5], -0.75)
+            nc.vector.memset(zc[:, :, :, :, 4:5], -0.75)
 
         def w_int(ch):
             if not ok(ch):
@@ -120,63 +128,53 @@ def tile_detect_v_kernel(tc, x0, x1, W0, b0, W1, b1, z0, grad_out, out_0, out_1)
         def p3(ch):
             if not ok(ch):
                 return
-            dn = work.tile([P, 4, 2, 256], BF16, name="dn", align_bytes=64)
+            zc, gc_in = zc_of(ch)
+            dn = work.tile([P, 2, 2, 2, 256], BF16, name="dn", align_bytes=64)
             for a in range(2):
-                nc.vector.scalar_tensor_tensor(out=dn[:, :, a, :], in0=zs[ch][:, a], scalar=0.25, in1=gs[ch][:, a],
+                nc.vector.scalar_tensor_tensor(out=dn[:, :, :, a, :], in0=zc[:, :, a], scalar=0.25, in1=gc_in[:, :, a],
                                                op0=ALU.subtract, op1=ALU.mult)
             dns[ch] = dn
 
         def spec(ch):
             if not ok(ch):
                 return
-            wsh, hsh = SHAPES[ch // 3]
+            zc, gc_in = zc_of(ch)
             ex = exs.pop(ch)
-            gt = gs.pop(ch)
-            zs.pop(ch)
-            dnv = dns[ch][:].rearrange("p j a f -> p a j f")
-            nc.vector.scalar_tensor_tensor(out=dnv[:, :, :, 2:3], in0=ex[:, :, :, 0:1], scalar=-wsh,
-                                           in1=gt[:, :, :, 2:3], op0=ALU.mult, op1=ALU.mult)
-            nc.vector.scalar_tensor_tensor(out=dnv[:, :, :, 3:4], in0=ex[:, :, :, 1:2], scalar=-hsh,
-                                           in1=gt[:, :, :, 3:4], op0=ALU.mult, op1=ALU.mult)
+            dn = dns[ch]
+            for g in range(2):
+                dnv = dn[:, g].rearrange("p j a f -> p a j f")
+                for k in range(2):
+                    nc.vector.scalar_tensor_tensor(out=dnv[:, :, :, 2 + k : 3 + k], in0=ex[:, g, :, :, k : k + 1],
+                                                   scalar=-SHAPES[ch // 3][k], in1=gc_in[:, g, :, :, 2 + k : 3 + k],
+                                                   op0=ALU.mult, op1=ALU.mult)
 
         def t1(ch):
             if not ok(ch):
                 return
-            dw = dns[ch][:].rearrange("p j a f -> p (j a f)").bitcast(F32)
+            dw = dns.pop(ch)[:].rearrange("p g j a f -> p (g j a f)").bitcast(F32)
             pair = []
-            for h in range(2):
+            for g in range(2):
                 tp = tpp.tile([P, 2, 2, P], F32, name="tp")
-                for k in range(2):
-                    j = 2 * h + k
-                    for u in range(2):
-                        nc.tensor.transpose(tp[:, k, u, :], dw[:, 256 * j + u : 256 * (j + 1) : 2], ident[:])
+                for u in range(2):
+                    for j in range(2):
+                        sl = 2 * g + j
+                        nc.tensor.transpose(tp[:, u, j, :], dw[:, 256 * sl + u : 256 * (sl + 1) : 2], perm[:])
                 pair.append(tp)
             tps[ch] = pair
 
-        def a_int(ch):
+        def tp_out(ch, g, on_vector):
             if not ok(ch):
                 return
-            ai = work.tile([P, 512, 4], BF16, name="ai", align_bytes=64)
-            nc.vector.tensor_copy(out=ai[:], in_=dns.pop(ch)[:].rearrange("p j a f -> p (a f) j"))
-            ais[ch] = ai
-
-        def tp_out(ch):
-            if not ok(ch):
-                return
-            gg = work.tile([P, 4, P, 4], BF16, name="gg", align_bytes=64)
+            if g == 0:
+                gg = work.tile([P, 4, P, 4], BF16, name="gg", align_bytes=64)
+                ggs[ch] = gg
+            gg = ggs[ch]
             ggw = gg[:].rearrange("p j r t -> p (j r t)").bitcast(F32).rearrange("p (j r u) -> p j r u", j=4, r=128, u=2)
-            pair = tps.pop(ch)
-            nc.scalar.copy(out=ggw[:, 0:2], in_=pair[0][:].rearrange("p k u r -> p k r u"))
-            nc.vector.tensor_copy(out=ggw[:, 2:4], in_=pair[1][:].rearrange("p k u r -> p k r u"))
-            ggs[ch] = gg
-
-        def a_quant(ch):
-            if not ok(ch):
-                return
-            ac = codes.tile([P, 512], U32, name="ac", align_bytes=64)
-            asc = codes.tile([P, 512], U8, name="asc", align_bytes=64)
-            nc.vector.quantize_mx(out=ac[:].bitcast(E5X4), scales=asc[:], in_=ais.pop(ch)[:].rearrange("p o j -> p (o j)"))
-            acs[ch] = (ac, asc)
+            src = tps[ch][g][:].rearrange("p u j (b m) -> p (j b) m u", b=2)
+            if on_vector:
+                nc.vector.tensor_copy(out=ggw[:, :, 64 * g : 64 * g + 64, :], in_=src)
+            else:
+                nc.scalar.copy(out=ggw[:, :, 64 * g : 64 * g + 64, :], in_=src)
 
         def g_quant(ch):
             if not ok(ch):
@@ -185,6 +183,39 @@ def tile_detect_v_kernel(tc, x0, x1, W0, b0, W1, b1, z0, grad_out, out_0, out_1)
             gsc = codes.tile([P, 512], U8, name="gsc", align_bytes=64)
             nc.vector.quantize_mx(out=gc[:].bitcast(E5X4), scales=gsc[:], in_=ggs.pop(ch)[:].rearrange("p j r t -> p (j r t)"))
             gcs[ch] = (gc, gsc)
+
+        def t_y(ch):
+            if not ok(ch):
+                return
+            gw = ggs[ch][:].rearrange("p j r t -> p (j r t)").bitcast(F32)
+            pair = []
+            for u in range(2):
+                ty = tpp.tile([P, 4, P], F32, name="tp")
+                for j in range(4):
+                    nc.tensor.transpose(ty[:, j, :], gw[:, 256 * j + u : 256 * (j + 1) : 2], ident[:])
+                pair.append(ty)
+            tys[ch] = pair
+
+        def ty_out(ch, u, on_vector):
+            if not ok(ch):
+                return
+            if u == 0:
+                ai = work.tile([P, 2, 2, P, 4], BF16, name="ai", align_bytes=64)
+                ais[ch] = ai
+            ai = ais[ch]
+            src = tys[ch][u][:].rearrange("m j p -> m (j p)").bitcast(BF16).rearrange("m (j p e) -> m e p j", j=4, p=128, e=2)
+            if on_vector:
+                nc.vector.tensor_copy(out=ai[:, u], in_=src)
+            else:
+                nc.scalar.copy(out=ai[:, u], in_=src)
+
+        def a_quant(ch):
+            if not ok(ch):
+                return
+            ac = codes.tile([P, 512], U32, name="ac", align_bytes=64)
+            asc = codes.tile([P, 512], U8, name="asc", align_bytes=64)
+            nc.vector.quantize_mx(out=ac[:].bitcast(E5X4), scales=asc[:], in_=ais.pop(ch)[:].rearrange("m u e p j -> m (u e p j)"))
+            acs[ch] = (ac, asc)
 
         def mm1(ch, m):
             if not ok(ch):
@@ -212,8 +243,8 @@ def tile_detect_v_kernel(tc, x0, x1, W0, b0, W1, b1, z0, grad_out, out_0, out_1)
         def store(ch, half):
             if not ok(ch):
                 return
-            r0 = 512 * ch + 256 * half
-            nc.sync.dma_start(out=out_1[r0 : r0 + 256, :].rearrange("(m p) c -> p m c", m=2), in_=sts.pop((ch, half))[:])
+            dst = out_1[512 * ch : 512 * ch + 512, :].rearrange("(p t) c -> p t c", t=4)
+            nc.sync.dma_start(out=dst[:, 2 * half : 2 * half + 2, :], in_=sts.pop((ch, half))[:])
 
         def mm0(ch):
             if not ok(ch):
@@ -227,15 +258,15 @@ def tile_detect_v_kernel(tc, x0, x1, W0, b0, W1, b1, z0, grad_out, out_0, out_1)
                                     start=(ch == 0), stop=(ch == NCH - 1))
 
         def evict0(ct, on_vector):
-            o0 = stage.tile([P, P, 4], F32, name="o0")
-            src = acc[ct][:].rearrange("c (j r) -> c r j", j=4)
+            o0 = stage0.tile([P, P, 2, 2], F32, name="o0")
+            src = acc[ct][:].rearrange("c (j b m) -> c m b j", j=2, b=2)
             if on_vector:
                 nc.vector.tensor_scalar(out=o0[:], in0=src, scalar1=-1.0, scalar2=None, op0=ALU.mult)
             else:
                 nc.scalar.activation(out=o0[:], in_=src, func=ACT.Copy, scale=-1.0)
             nc.sync.dma_start(
                 out=out_0[:, 128 * ct : 128 * ct + 128, :, :].rearrange("b c gy gx -> c b (gy gx)"),
-                in_=o0[:].rearrange("c r j -> c (r j)").rearrange("c (b s) -> c b s", b=NB),
+                in_=o0[:].rearrange("c m b j -> c (m b j)").rearrange("c (i s) -> c i s", i=NB),
             )
 
         warm = const.tile([P, 1], F32, name="warm")
@@ -244,9 +275,12 @@ def tile_detect_v_kernel(tc, x0, x1, W0, b0, W1, b1, z0, grad_out, out_0, out_1)
         nc.scalar.activation(out=warm2[:], in_=warm[:], func=ACT.Exp)
         ident = const.tile([P, P], F32, name="ident")
         make_identity(nc, ident[:])
+        perm = const.tile([P, P], F32, name="perm")
+        nc.vector.tensor_copy(out=perm[:].rearrange("p (b m) -> p b m", b=2), in_=ident[:].rearrange("p (m b) -> p b m", b=2))
         acc = [accp.tile([P, 512], F32, name="acc%d" % ct) for ct in range(4)]
 
         load(0)
+        load(1)
         load_w(0)
         xraw = const.tile([P, 4, 512], BF16, name="xraw")
         for cb in range(4):
@@ -254,62 +288,66 @@ def tile_detect_v_kernel(tc, x0, x1, W0, b0, W1, b1, z0, grad_out, out_0, out_1)
                 out=xraw[:, cb, :].rearrange("c (b s) -> c b s", b=NB),
                 in_=x0[:, 128 * cb : 128 * cb + 128, :, :].rearrange("b c gy gx -> c b (gy gx)"),
             )
-        load_w(1)
-        load(1)
-        load_w(2)
         load(2)
-
-        act_e(0)
-        w_int(0)
-        xw = xraw[:].rearrange("c cb t -> c (cb t)").bitcast(F32)
+        load_w(1)
         xg = const.tile([P, C, 4], BF16, name="xg", align_bytes=64)
-        xgw = xg[:].rearrange("p c t -> p (c t)").bitcast(F32).rearrange("p (cb c u) -> p cb c u", cb=4, c=128, u=2)
-        for h in range(2):
-            tp = tpp.tile([P, 2, 2, P], F32, name="tp")
-            for k in range(2):
-                cb = 2 * h + k
-                for u in range(2):
-                    nc.tensor.transpose(tp[:, k, u, :], xw[:, 256 * cb + u : 256 * (cb + 1) : 2], ident[:])
-            nc.vector.tensor_copy(out=xgw[:, 2 * h : 2 * h + 2], in_=tp[:].rearrange("p k u r -> p k r u"))
-        w_quant(0)
         xc = const.tile([P, C], U32, name="xc", align_bytes=64)
         xs = const.tile([P, C], U8, name="xs", align_bytes=64)
-        nc.vector.quantize_mx(out=xc[:].bitcast(E4X4), scales=xs[:], in_=xg[:].rearrange("p c t -> p (c t)"))
+
+        def x_prep():
+            xw = xraw[:].rearrange("c cb t -> c (cb t)").bitcast(F32)
+            for h in range(2):
+                xt = o1p.tile([P, 2, 2, P], F32, name="o1")
+                for k2 in range(2):
+                    cb = 2 * h + k2
+                    for u in range(2):
+                        nc.tensor.transpose(xt[:, k2, u, :], xw[:, 256 * cb + u : 256 * (cb + 1) : 2], ident[:])
+                for k2 in range(2):
+                    cb = 2 * h + k2
+                    src = xt[:, k2].rearrange("p u c -> p (u c)").bitcast(BF16).rearrange("p (u c e) -> p c e u", u=2, c=128, e=2)
+                    nc.vector.tensor_copy(out=xg[:, 128 * cb : 128 * cb + 128, :].rearrange("p c (e u) -> p c e u", e=2), in_=src)
+            nc.vector.quantize_mx(out=xc[:].bitcast(E4X4), scales=xs[:], in_=xg[:].rearrange("p c t -> p (c t)"))
+
+        act_e(0)
         patches(0)
 
-        for k in range(0, NCH + 1):
-            last = k - 1 == NCH - 1
-            store(k - 2, 0)
-            store(k - 2, 1)
-            load_w(k + 3)
+        stored = -1
+        for k in range(0, NCH + 3):
             load(k + 3)
+            load_w(k + 2)
+            if k >= 6:
+                for c in range(stored + 1, min(k - 3, NCH - 1) + 1):
+                    store(c, 0)
+                    store(c, 1)
+                    stored = c
+            tail = k >= NCH
+            ty_out(k - 1, 0, False)
+            ty_out(k - 1, 1, tail)
+            evict(k - 2, 0, False)
+            evict(k - 2, 1, False)
             act_e(k + 1)
             p3(k)
-            if k == 0:
-                w_int(1)
-            w_quant(k + 1)
+            g_quant(k - 1)
             spec(k)
             t1(k)
-            w_int(k + 2)
-            a_int(k)
-            tp_out(k)
-            a_quant(k)
-            evict(k - 1, 0, False)
-            mm1(k - 1, 2)
-            evict(k - 1, 1, last)
-            mm1(k - 1, 3)
-            if last:
-                store(k - 1, 0)
+            w_int(k - 1)
+            mm1(k - 2, 2)
+            mm1(k - 2, 3)
+            tp_out(k, 0, k != NCH - 1)
+            tp_out(k, 1, True)
+            t_y(k)
+            a_quant(k - 1)
+            w_quant(k - 1)
+            mm0(k - 1)
+            if k == 1:
+                x_prep()
+            evict(k - 2, 2, True)
+            evict(k - 2, 3, True)
+            mm1(k - 1, 0)
+            mm1(k - 1, 1)
+            patches(k + 1)
+            if k == NCH:
                 evict0(0, False)
                 evict0(1, True)
-            evict(k - 1, 2, False)
-            evict(k - 1, 3, last)
-            if last:
-                store(k - 1, 1)
                 evict0(2, False)
                 evict0(3, True)
-            patches(k + 1)
-            g_quant(k)
-            mm1(k, 0)
-            mm1(k, 1)
-            mm0(k)

@@ -23,9 +23,6 @@ FLOPS = 2 * 2 * 512 * 4608 * 512
 BYTES = 524288 + 4718592 + 9437184 + 4718592 + 1048576 + 9437184
 
 
-IMG_ORDER = (0, 2, 1, 3, 4, 6, 5, 7)
-
-
 def tile_detect_v_kernel(tc, x0, x1, W0, b0, W1, b1, z0, grad_out, out_0, out_1):
     nc = tc.nc
     with ExitStack() as ctx:
@@ -35,7 +32,7 @@ def tile_detect_v_kernel(tc, x0, x1, W0, b0, W1, b1, z0, grad_out, out_0, out_1)
         wpool = ctx.enter_context(tc.tile_pool(name="wpool", bufs=3))
         work = ctx.enter_context(tc.tile_pool(name="work", bufs=2))
         codes = ctx.enter_context(tc.tile_pool(name="codes", bufs=3))
-        stage = ctx.enter_context(tc.tile_pool(name="stage", bufs=18))
+        stage = ctx.enter_context(tc.tile_pool(name="stage", bufs=12))
         stage0 = ctx.enter_context(tc.tile_pool(name="stage0", bufs=4))
         accp = ctx.enter_context(tc.psum_pool(name="accp", bufs=1))
         tpp = ctx.enter_context(tc.psum_pool(name="tpp", bufs=2))
@@ -61,25 +58,34 @@ def tile_detect_v_kernel(tc, x0, x1, W0, b0, W1, b1, z0, grad_out, out_0, out_1)
         def ok(ch):
             return 0 <= ch < NCH
 
-        def load(ch):
+        def load_part(ch, g, what):
             if not ok(ch):
                 return
-            zt = zpool.tile([P, 2, 2, 2, 256], F32, name="zt")
-            gt = gpool.tile([P, 2, 2, 2, 256], BF16, name="gt")
-            for b in IMG_ORDER:
-                lo = 32 * (b % 4)
+            if what == 0:
+                if g == 0:
+                    zt = zpool.tile([P, 2, 2, 2, 256], F32, name="zt")
+                    zg[ch] = zt
+                dst, src = zg[ch], z0
+            else:
+                if g == 0:
+                    gt = gpool.tile([P, 2, 2, 2, 256], BF16, name="gt")
+                    gg_in[ch] = gt
+                dst, src = gg_in[ch], grad_out
+            for b3 in (0, 2, 1, 3):
                 nc.sync.dma_start(
-                    out=zt[lo : lo + 32, b // 4],
-                    in_=z0[b, 128 * ch : 128 * ch + 128, :].rearrange("(a q j) f -> q a j f", a=2, q=32, j=2),
+                    out=dst[32 * b3 : 32 * b3 + 32, g],
+                    in_=src[4 * g + b3, 128 * ch : 128 * ch + 128, :].rearrange("(a q j) f -> q a j f", a=2, q=32, j=2),
                 )
-            for b in IMG_ORDER:
-                lo = 32 * (b % 4)
-                nc.sync.dma_start(
-                    out=gt[lo : lo + 32, b // 4],
-                    in_=grad_out[b, 128 * ch : 128 * ch + 128, :].rearrange("(a q j) f -> q a j f", a=2, q=32, j=2),
-                )
-            zg[ch] = zt
-            gg_in[ch] = gt
+
+        def load(ch, by_half):
+            if by_half:
+                for g in range(2):
+                    load_part(ch, g, 0)
+                    load_part(ch, g, 1)
+            else:
+                for what in range(2):
+                    for g in range(2):
+                        load_part(ch, g, what)
 
         def zc_of(ch):
             return zg[ch][:], gg_in[ch][:]
@@ -91,24 +97,33 @@ def tile_detect_v_kernel(tc, x0, x1, W0, b0, W1, b1, z0, grad_out, out_0, out_1)
             nc.sync.dma_start(out=wraw[:], in_=W0[512 * ch : 512 * ch + 512, :].rearrange("(p t) c -> p t c", t=4))
             ws[ch] = wraw
 
-        def act_e(ch):
+        def act_e(ch, by_half):
             if not ok(ch):
                 return
             zc, gc_in = zc_of(ch)
             ex = work.tile([P, 2, 2, 2, 2], F32, name="ex")
-            nc.scalar.activation(out=ex[:], in_=zc[:, :, :, :, 2:4], func=ACT.Exp)
-            zf = zc.rearrange("p g a j f -> p g (a j f)")
-            nc.scalar.activation(out=zf, in_=zf, func=ACT.Tanh, scale=0.5)
-            nc.scalar.activation(out=zf, in_=zf, func=ACT.Square, scale=0.5)
             exs[ch] = ex
 
-        def patches(ch):
-            if not ok(ch):
-                return
-            zc, gc_in = zc_of(ch)
-            nc.vector.tensor_scalar(out=zc[:, :, :, :, 0:2], in0=zc[:, :, :, :, 0:2], scalar1=9.6, scalar2=-2.15,
-                                    op0=ALU.mult, op1=ALU.add)
-            nc.vector.memset(zc[:, :, :, :, 4:5], -0.75)
+            def step(s, g):
+                zf = zc[:, g].rearrange("p a j f -> p (a j f)")
+                if s == 0:
+                    nc.scalar.activation(out=ex[:, g], in_=zc[:, g, :, :, 2:4], func=ACT.Exp)
+                elif s == 1:
+                    nc.scalar.activation(out=zf, in_=zf, func=ACT.Tanh, scale=0.5)
+                elif s == 2:
+                    nc.scalar.activation(out=zf, in_=zf, func=ACT.Square, scale=0.5)
+                else:
+                    nc.scalar.activation(out=zc[:, g, :, :, 0:2], in_=zc[:, g, :, :, 0:2], func=ACT.Copy, scale=9.6, bias=-2.15)
+                    nc.scalar.activation(out=zc[:, g, :, :, 4:5], in_=zc[:, g, :, :, 4:5], func=ACT.Copy, scale=0.0, bias=-0.75)
+
+            if by_half:
+                for g in range(2):
+                    for s in range(4):
+                        step(s, g)
+            else:
+                for s in range(4):
+                    for g in range(2):
+                        step(s, g)
 
         def w_int(ch):
             if not ok(ch):
@@ -135,32 +150,37 @@ def tile_detect_v_kernel(tc, x0, x1, W0, b0, W1, b1, z0, grad_out, out_0, out_1)
                                                op0=ALU.subtract, op1=ALU.mult)
             dns[ch] = dn
 
-        def spec(ch):
+        def p3_half(ch, g):
+            zc, gc_in = zc_of(ch)
+            if g == 0:
+                dn = work.tile([P, 2, 2, 2, 256], BF16, name="dn", align_bytes=64)
+                dns[ch] = dn
+            dn = dns[ch]
+            for a in range(2):
+                nc.vector.scalar_tensor_tensor(out=dn[:, g, :, a, :], in0=zc[:, g, a], scalar=0.25, in1=gc_in[:, g, a],
+                                               op0=ALU.subtract, op1=ALU.mult)
+
+        def spec(ch, g):
             if not ok(ch):
                 return
             zc, gc_in = zc_of(ch)
-            ex = exs.pop(ch)
-            dn = dns[ch]
-            for g in range(2):
-                dnv = dn[:, g].rearrange("p j a f -> p a j f")
-                for k in range(2):
-                    nc.vector.scalar_tensor_tensor(out=dnv[:, :, :, 2 + k : 3 + k], in0=ex[:, g, :, :, k : k + 1],
-                                                   scalar=-SHAPES[ch // 3][k], in1=gc_in[:, g, :, :, 2 + k : 3 + k],
-                                                   op0=ALU.mult, op1=ALU.mult)
+            ex = exs[ch]
+            dnv = dns[ch][:, g].rearrange("p j a f -> p a j f")
+            for k2 in range(2):
+                nc.vector.scalar_tensor_tensor(out=dnv[:, :, :, 2 + k2 : 3 + k2], in0=ex[:, g, :, :, k2 : k2 + 1],
+                                               scalar=-SHAPES[ch // 3][k2], in1=gc_in[:, g, :, :, 2 + k2 : 3 + k2],
+                                               op0=ALU.mult, op1=ALU.mult)
 
-        def t1(ch):
+        def t1(ch, g):
             if not ok(ch):
                 return
-            dw = dns.pop(ch)[:].rearrange("p g j a f -> p (g j a f)").bitcast(F32)
-            pair = []
-            for g in range(2):
-                tp = tpp.tile([P, 2, 2, P], F32, name="tp")
-                for u in range(2):
-                    for j in range(2):
-                        sl = 2 * g + j
-                        nc.tensor.transpose(tp[:, u, j, :], dw[:, 256 * sl + u : 256 * (sl + 1) : 2], perm[:])
-                pair.append(tp)
-            tps[ch] = pair
+            dw = dns[ch][:].rearrange("p g j a f -> p (g j a f)").bitcast(F32)
+            tp = tpp.tile([P, 2, 2, P], F32, name="tp")
+            for u in range(2):
+                for j in range(2):
+                    sl = 2 * g + j
+                    nc.tensor.transpose(tp[:, u, j, :], dw[:, 256 * sl + u : 256 * (sl + 1) : 2], perm[:])
+            tps[(ch, g)] = tp
 
         def tp_out(ch, g, on_vector):
             if not ok(ch):
@@ -170,7 +190,7 @@ def tile_detect_v_kernel(tc, x0, x1, W0, b0, W1, b1, z0, grad_out, out_0, out_1)
                 ggs[ch] = gg
             gg = ggs[ch]
             ggw = gg[:].rearrange("p j r t -> p (j r t)").bitcast(F32).rearrange("p (j r u) -> p j r u", j=4, r=128, u=2)
-            src = tps[ch][g][:].rearrange("p u j (b m) -> p (j b) m u", b=2)
+            src = tps.pop((ch, g))[:].rearrange("p u j (b m) -> p (j b) m u", b=2)
             if on_vector:
                 nc.vector.tensor_copy(out=ggw[:, :, 64 * g : 64 * g + 64, :], in_=src)
             else:
@@ -240,11 +260,11 @@ def tile_detect_v_kernel(tc, x0, x1, W0, b0, W1, b1, z0, grad_out, out_0, out_1)
             else:
                 nc.scalar.activation(out=st[:, m % 2, :], in_=o1[:], func=ACT.Copy, scale=-1.0)
 
-        def store(ch, half):
+        def store(ch, half, ring):
             if not ok(ch):
                 return
             dst = out_1[512 * ch : 512 * ch + 512, :].rearrange("(p t) c -> p t c", t=4)
-            nc.sync.dma_start(out=dst[:, 2 * half : 2 * half + 2, :], in_=sts.pop((ch, half))[:])
+            ring.dma_start(out=dst[:, 2 * half : 2 * half + 2, :], in_=sts.pop((ch, half))[:])
 
         def mm0(ch):
             if not ok(ch):
@@ -279,8 +299,8 @@ def tile_detect_v_kernel(tc, x0, x1, W0, b0, W1, b1, z0, grad_out, out_0, out_1)
         nc.vector.tensor_copy(out=perm[:].rearrange("p (b m) -> p b m", b=2), in_=ident[:].rearrange("p (m b) -> p b m", b=2))
         acc = [accp.tile([P, 512], F32, name="acc%d" % ct) for ct in range(4)]
 
-        load(0)
-        load(1)
+        load(0, True)
+        load(1, False)
         load_w(0)
         xraw = const.tile([P, 4, 512], BF16, name="xraw")
         for cb in range(4):
@@ -288,7 +308,7 @@ def tile_detect_v_kernel(tc, x0, x1, W0, b0, W1, b1, z0, grad_out, out_0, out_1)
                 out=xraw[:, cb, :].rearrange("c (b s) -> c b s", b=NB),
                 in_=x0[:, 128 * cb : 128 * cb + 128, :, :].rearrange("b c gy gx -> c b (gy gx)"),
             )
-        load(2)
+        load(2, False)
         load_w(1)
         xg = const.tile([P, C, 4], BF16, name="xg", align_bytes=64)
         xc = const.tile([P, C], U32, name="xc", align_bytes=64)
@@ -308,28 +328,35 @@ def tile_detect_v_kernel(tc, x0, x1, W0, b0, W1, b1, z0, grad_out, out_0, out_1)
                     nc.vector.tensor_copy(out=xg[:, 128 * cb : 128 * cb + 128, :].rearrange("p c (e u) -> p c e u", e=2), in_=src)
             nc.vector.quantize_mx(out=xc[:].bitcast(E4X4), scales=xs[:], in_=xg[:].rearrange("p c t -> p (c t)"))
 
-        act_e(0)
-        patches(0)
+        act_e(0, True)
 
-        stored = -1
         for k in range(0, NCH + 3):
-            load(k + 3)
+            load(k + 3, k + 3 == NCH - 1)
             load_w(k + 2)
-            if k >= 6:
-                for c in range(stored + 1, min(k - 3, NCH - 1) + 1):
-                    store(c, 0)
-                    store(c, 1)
-                    stored = c
+            late = k >= NCH - 1
+            ring = nc.sync if late else nc.gpsimd
             tail = k >= NCH
             ty_out(k - 1, 0, False)
             ty_out(k - 1, 1, tail)
             evict(k - 2, 0, False)
             evict(k - 2, 1, False)
-            act_e(k + 1)
-            p3(k)
-            g_quant(k - 1)
-            spec(k)
-            t1(k)
+            store(k - 2, 0, ring)
+            act_e(k + 1, k + 1 == NCH - 1)
+            if k == 0 or k == NCH - 1:
+                p3_half(k, 0)
+                spec(k, 0)
+                t1(k, 0)
+                p3_half(k, 1)
+                g_quant(k - 1)
+                spec(k, 1)
+                t1(k, 1)
+            else:
+                p3(k)
+                g_quant(k - 1)
+                spec(k, 0)
+                spec(k, 1)
+                t1(k, 0)
+                t1(k, 1)
             w_int(k - 1)
             mm1(k - 2, 2)
             mm1(k - 2, 3)
@@ -341,13 +368,14 @@ def tile_detect_v_kernel(tc, x0, x1, W0, b0, W1, b1, z0, grad_out, out_0, out_1)
             mm0(k - 1)
             if k == 1:
                 x_prep()
-            evict(k - 2, 2, True)
-            evict(k - 2, 3, True)
-            mm1(k - 1, 0)
-            mm1(k - 1, 1)
-            patches(k + 1)
             if k == NCH:
                 evict0(0, False)
                 evict0(1, True)
+            evict(k - 2, 2, True)
+            evict(k - 2, 3, True)
+            store(k - 2, 1, ring)
+            mm1(k - 1, 0)
+            mm1(k - 1, 1)
+            if k == NCH:
                 evict0(2, False)
                 evict0(3, True)

@@ -19,6 +19,11 @@ C = 512
 SHAPES = ((10.0, 13.0), (16.0, 30.0), (33.0, 23.0))
 B_ORDER = (0, 1, 4, 5, 2, 3, 6, 7)
 
+ZGROUPS = ((0, 1), (1, 2), (3, 2), (5, 2), (7, 1), (8, 1))
+ZGROUP_OF = (0, 1, 1, 2, 2, 3, 3, 4, 5)
+GGROUPS = ((0, 1), (1, 2), (3, 2), (5, 2), (7, 2))
+GGROUP_OF = (0, 1, 1, 2, 2, 3, 3, 4, 4)
+
 FLOPS = 2 * 2 * 512 * 4608 * 512
 BYTES = 524288 + 4718592 + 9437184 + 4718592 + 1048576 + 9437184
 
@@ -27,9 +32,9 @@ def tile_detect_v_kernel(tc, x0, x1, W0, b0, W1, b1, z0, grad_out, out_0, out_1)
     nc = tc.nc
     with ExitStack() as ctx:
         const = ctx.enter_context(tc.tile_pool(name="const", bufs=1))
-        zpool = ctx.enter_context(tc.tile_pool(name="zpool", bufs=4))
-        gpool = ctx.enter_context(tc.tile_pool(name="gpool", bufs=4))
-        wpool = ctx.enter_context(tc.tile_pool(name="wpool", bufs=3))
+        zpool = ctx.enter_context(tc.tile_pool(name="zpool", bufs=3))
+        gpool = ctx.enter_context(tc.tile_pool(name="gpool", bufs=3))
+        wpool = ctx.enter_context(tc.tile_pool(name="wpool", bufs=4))
         work = ctx.enter_context(tc.tile_pool(name="work", bufs=2))
         codes = ctx.enter_context(tc.tile_pool(name="codes", bufs=3))
         stage = ctx.enter_context(tc.tile_pool(name="stage", bufs=12))
@@ -58,37 +63,35 @@ def tile_detect_v_kernel(tc, x0, x1, W0, b0, W1, b1, z0, grad_out, out_0, out_1)
         def ok(ch):
             return 0 <= ch < NCH
 
-        def load_part(ch, g, what):
-            if not ok(ch):
-                return
+        def load_part(gi, g, what):
             if what == 0:
                 if g == 0:
-                    zt = zpool.tile([P, 2, 2, 2, 256], F32, name="zt")
-                    zg[ch] = zt
-                dst, src = zg[ch], z0
+                    zt = zpool.tile([P, 2, 4, 2, 256], F32, name="zt")
+                    zg[gi] = zt
+                dst, src = zg[gi], z0
+                c0, n = ZGROUPS[gi]
             else:
                 if g == 0:
-                    gt = gpool.tile([P, 2, 2, 2, 256], BF16, name="gt")
-                    gg_in[ch] = gt
-                dst, src = gg_in[ch], grad_out
+                    gt = gpool.tile([P, 2, 4, 2, 256], BF16, name="gt")
+                    gg_in[gi] = gt
+                dst, src = gg_in[gi], grad_out
+                c0, n = GGROUPS[gi]
             for b3 in (0, 2, 1, 3):
                 nc.sync.dma_start(
-                    out=dst[32 * b3 : 32 * b3 + 32, g],
-                    in_=src[4 * g + b3, 128 * ch : 128 * ch + 128, :].rearrange("(a q j) f -> q a j f", a=2, q=32, j=2),
+                    out=dst[32 * b3 : 32 * b3 + 32, g, 0 : 2 * n],
+                    in_=src[4 * g + b3, 128 * c0 : 128 * (c0 + n), :].rearrange("(a q j) f -> q a j f", a=2 * n, q=32, j=2),
                 )
 
-        def load(ch, by_half):
-            if by_half:
-                for g in range(2):
-                    load_part(ch, g, 0)
-                    load_part(ch, g, 1)
-            else:
-                for what in range(2):
-                    for g in range(2):
-                        load_part(ch, g, what)
+        def load_group(gi, what):
+            load_part(gi, 0, what)
+            load_part(gi, 1, what)
 
         def zc_of(ch):
-            return zg[ch][:], gg_in[ch][:]
+            zi = ZGROUP_OF[ch]
+            gi = GGROUP_OF[ch]
+            lz = 2 * (ch - ZGROUPS[zi][0])
+            lg = 2 * (ch - GGROUPS[gi][0])
+            return zg[zi][:, :, lz : lz + 2], gg_in[gi][:, :, lg : lg + 2]
 
         def load_w(ch):
             if not ok(ch):
@@ -299,39 +302,48 @@ def tile_detect_v_kernel(tc, x0, x1, W0, b0, W1, b1, z0, grad_out, out_0, out_1)
         nc.vector.tensor_copy(out=perm[:].rearrange("p (b m) -> p b m", b=2), in_=ident[:].rearrange("p (m b) -> p b m", b=2))
         acc = [accp.tile([P, 512], F32, name="acc%d" % ct) for ct in range(4)]
 
-        load(0, True)
-        load(1, False)
+        xraw = const.tile([P, NB, 4, 64], BF16, name="xraw")
+        nc.sync.dma_start(out=xraw[:], in_=x0.rearrange("b (q cl) gy gx -> q b cl (gy gx)", cl=4))
+        for g in range(2):
+            load_part(0, g, 0)
+            load_part(0, g, 1)
+        load_group(1, 0)
+        load_group(1, 1)
         load_w(0)
-        xraw = const.tile([P, 4, 512], BF16, name="xraw")
-        for cb in range(4):
-            nc.sync.dma_start(
-                out=xraw[:, cb, :].rearrange("c (b s) -> c b s", b=NB),
-                in_=x0[:, 128 * cb : 128 * cb + 128, :, :].rearrange("b c gy gx -> c b (gy gx)"),
-            )
-        load(2, False)
+        load_group(2, 0)
         load_w(1)
+        load_group(2, 1)
+        xr = const.tile([P, 4, 512], BF16, name="xr")
         xg = const.tile([P, C, 4], BF16, name="xg", align_bytes=64)
         xc = const.tile([P, C], U32, name="xc", align_bytes=64)
         xs = const.tile([P, C], U8, name="xs", align_bytes=64)
 
-        def x_prep():
-            xw = xraw[:].rearrange("c cb t -> c (cb t)").bitcast(F32)
-            for h in range(2):
-                xt = o1p.tile([P, 2, 2, P], F32, name="o1")
-                for k2 in range(2):
-                    cb = 2 * h + k2
-                    for u in range(2):
-                        nc.tensor.transpose(xt[:, k2, u, :], xw[:, 256 * cb + u : 256 * (cb + 1) : 2], ident[:])
-                for k2 in range(2):
-                    cb = 2 * h + k2
-                    src = xt[:, k2].rearrange("p u c -> p (u c)").bitcast(BF16).rearrange("p (u c e) -> p c e u", u=2, c=128, e=2)
-                    nc.vector.tensor_copy(out=xg[:, 128 * cb : 128 * cb + 128, :].rearrange("p c (e u) -> p c e u", e=2), in_=src)
-            nc.vector.quantize_mx(out=xc[:].bitcast(E4X4), scales=xs[:], in_=xg[:].rearrange("p c t -> p (c t)"))
-
         act_e(0, True)
 
+        nc.vector.tensor_copy(out=xr[:].rearrange("q cl (b s) -> q cl b s", b=NB), in_=xraw[:].rearrange("q b cl s -> q cl b s"))
+        xw = xr[:].rearrange("q cl t -> q (cl t)").bitcast(F32)
+        xgv = xg[:].rearrange("p (q cl) t -> p cl q t", cl=4)
+        for h in range(2):
+            xt = o1p.tile([P, 2, 2, P], F32, name="o1")
+            for k2 in range(2):
+                cl = 2 * h + k2
+                for u in range(2):
+                    nc.tensor.transpose(xt[:, k2, u, :], xw[:, 256 * cl + u : 256 * (cl + 1) : 2], ident[:])
+            for k2 in range(2):
+                cl = 2 * h + k2
+                src = xt[:, k2].rearrange("p u q -> p (u q)").bitcast(BF16).rearrange("p (u q e) -> p q e u", u=2, q=128, e=2)
+                nc.vector.tensor_copy(out=xgv[:, cl].rearrange("p q (e u) -> p q e u", e=2), in_=src)
+        nc.vector.quantize_mx(out=xc[:].bitcast(E4X4), scales=xs[:], in_=xg[:].rearrange("p c t -> p (c t)"))
+
         for k in range(0, NCH + 3):
-            load(k + 3, k + 3 == NCH - 1)
+            if k == 1:
+                load_group(3, 0)
+                load_group(3, 1)
+            if k == 3:
+                load_group(4, 1)
+                load_group(4, 0)
+            if k == 5:
+                load_group(5, 0)
             load_w(k + 2)
             late = k >= NCH - 1
             ring = nc.sync if late else nc.gpsimd
@@ -366,8 +378,6 @@ def tile_detect_v_kernel(tc, x0, x1, W0, b0, W1, b1, z0, grad_out, out_0, out_1)
             a_quant(k - 1)
             w_quant(k - 1)
             mm0(k - 1)
-            if k == 1:
-                x_prep()
             if k == NCH:
                 evict0(0, False)
                 evict0(1, True)

from contextlib import ExitStack

import concourse.mybir as mybir
from concourse.masks import make_identity

F32 = mybir.dt.float32
BF16 = mybir.dt.bfloat16
U32 = mybir.dt.uint32
U8 = mybir.dt.uint8
E4X4 = mybir.dt.float8_e4m3fn_x4
E5X4 = mybir.dt.float8_e5m2_x4
ALU = mybir.AluOpType
ACT = mybir.ActivationFunctionType

P = 128
NB = 8
NCH = 9
C = 512
SHAPES = ((10.0, 13.0), (16.0, 30.0), (33.0, 23.0))
B_ORDER = (0, 1, 4, 5, 2, 3, 6, 7)

ZGROUPS = ((0, 1), (1, 2), (3, 2), (5, 2), (7, 1), (8, 1))
ZGROUP_OF = (0, 1, 1, 2, 2, 3, 3, 4, 5)
GGROUPS = ((0, 1), (1, 2), (3, 2), (5, 2), (7, 2))
GGROUP_OF = (0, 1, 1, 2, 2, 3, 3, 4, 4)

FLOPS = 2 * 2 * 512 * 4608 * 512
BYTES = 524288 + 4718592 + 9437184 + 4718592 + 1048576 + 9437184


def tile_detect_v_kernel(tc, x0, x1, W0, b0, W1, b1, z0, grad_out, out_0, out_1):
    nc = tc.nc
    with ExitStack() as ctx:
        const = ctx.enter_context(tc.tile_pool(name="const", bufs=1))
        zpool = ctx.enter_context(tc.tile_pool(name="zpool", bufs=3))
        gpool = ctx.enter_context(tc.tile_pool(name="gpool", bufs=3))
        wpool = ctx.enter_context(tc.tile_pool(name="wpool", bufs=4))
        work = ctx.enter_context(tc.tile_pool(name="work", bufs=2))
        codes = ctx.enter_context(tc.tile_pool(name="codes", bufs=3))
        stage = ctx.enter_context(tc.tile_pool(name="stage", bufs=12))
        stage0 = ctx.enter_context(tc.tile_pool(name="stage0", bufs=4))
        accp = ctx.enter_context(tc.psum_pool(name="accp", bufs=1))
        tpp = ctx.enter_context(tc.psum_pool(name="tpp", bufs=2))
        o1p = ctx.enter_context(tc.psum_pool(name="o1p", bufs=2))
        ctx.enter_context(tc.manual_schedule())

        zg = {}
        gg_in = {}
        ws = {}
        exs = {}
        wgs = {}
        wcs = {}
        dns = {}
        tps = {}
        ggs = {}
        gcs = {}
        tys = {}
        ais = {}
        acs = {}
        o1s = {}
        sts = {}

        def ok(ch):
            return 0 <= ch < NCH

        def load_part(gi, g, what):
            if what == 0:
                if g == 0:
                    zt = zpool.tile([P, 2, 4, 2, 256], F32, name="zt")
                    zg[gi] = zt
                dst, src = zg[gi], z0
                c0, n = ZGROUPS[gi]
            else:
                if g == 0:
                    gt = gpool.tile([P, 2, 4, 2, 256], BF16, name="gt")
                    gg_in[gi] = gt
                dst, src = gg_in[gi], grad_out
                c0, n = GGROUPS[gi]
            for b3 in (0, 2, 1, 3):
                nc.sync.dma_start(
                    out=dst[32 * b3 : 32 * b3 + 32, g, 0 : 2 * n],
                    in_=src[4 * g + b3, 128 * c0 : 128 * (c0 + n), :].rearrange("(a q j) f -> q a j f", a=2 * n, q=32, j=2),
                )

        def load_group(gi, what):
            load_part(gi, 0, what)
            load_part(gi, 1, what)

        def zc_of(ch):
            zi = ZGROUP_OF[ch]
            gi = GGROUP_OF[ch]
            lz = 2 * (ch - ZGROUPS[zi][0])
            lg = 2 * (ch - GGROUPS[gi][0])
            return zg[zi][:, :, lz : lz + 2], gg_in[gi][:, :, lg : lg + 2]

        def load_w(ch):
            if not ok(ch):
                return
            wraw = wpool.tile([P, 4, C], BF16, name="wraw")
            nc.sync.dma_start(out=wraw[:], in_=W0[512 * ch : 512 * ch + 512, :].rearrange("(p t) c -> p t c", t=4))
            ws[ch] = wraw

        def act_e(ch, by_half):
            if not ok(ch):
                return
            zc, gc_in = zc_of(ch)
            ex = work.tile([P, 2, 2, 2, 2], F32, name="ex")
            exs[ch] = ex

            def step(s, g):
                zf = zc[:, g].rearrange("p a j f -> p (a j f)")
                if s == 0:
                    nc.scalar.activation(out=ex[:, g], in_=zc[:, g, :, :, 2:4], func=ACT.Exp)
                elif s == 1:
                    nc.scalar.activation(out=zf, in_=zf, func=ACT.Tanh, scale=0.5)
                elif s == 2:
                    nc.scalar.activation(out=zf, in_=zf, func=ACT.Square, scale=0.5)
                else:
                    nc.scalar.activation(out=zc[:, g, :, :, 0:2], in_=zc[:, g, :, :, 0:2], func=ACT.Copy, scale=9.6, bias=-2.15)
                    nc.scalar.activation(out=zc[:, g, :, :, 4:5], in_=zc[:, g, :, :, 4:5], func=ACT.Copy, scale=0.0, bias=-0.75)

            if by_half:
                for g in range(2):
                    for s in range(4):
                        step(s, g)
            else:
                for s in range(4):
                    for g in range(2):
                        step(s, g)

        def w_int(ch):
            if not ok(ch):
                return
            wg = work.tile([P, C, 4], BF16, name="wg", align_bytes=64)
            nc.vector.tensor_copy(out=wg[:], in_=ws.pop(ch)[:].rearrange("p t c -> p c t"))
            wgs[ch] = wg

        def w_quant(ch):
            if not ok(ch):
                return
            wc = codes.tile([P, C], U32, name="wc", align_bytes=64)
            wsc = codes.tile([P, C], U8, name="wsc", align_bytes=64)
            nc.vector.quantize_mx(out=wc[:].bitcast(E4X4), scales=wsc[:], in_=wgs.pop(ch)[:].rearrange("p c t -> p (c t)"))
            wcs[ch] = (wc, wsc)

        def p3(ch):
            if not ok(ch):
                return
            zc, gc_in = zc_of(ch)
            dn = work.tile([P, 2, 2, 2, 256], BF16, name="dn", align_bytes=64)
            for a in range(2):
                nc.vector.scalar_tensor_tensor(out=dn[:, :, :, a, :], in0=zc[:, :, a], scalar=0.25, in1=gc_in[:, :, a],
                                               op0=ALU.subtract, op1=ALU.mult)
            dns[ch] = dn

        def p3_half(ch, g):
            zc, gc_in = zc_of(ch)
            if g == 0:
                dn = work.tile([P, 2, 2, 2, 256], BF16, name="dn", align_bytes=64)
                dns[ch] = dn
            dn = dns[ch]
            for a in range(2):
                nc.vector.scalar_tensor_tensor(out=dn[:, g, :, a, :], in0=zc[:, g, a], scalar=0.25, in1=gc_in[:, g, a],
                                               op0=ALU.subtract, op1=ALU.mult)

        def spec(ch, g):
            if not ok(ch):
                return
            zc, gc_in = zc_of(ch)
            ex = exs[ch]
            dnv = dns[ch][:, g].rearrange("p j a f -> p a j f")
            for k2 in range(2):
                nc.vector.scalar_tensor_tensor(out=dnv[:, :, :, 2 + k2 : 3 + k2], in0=ex[:, g, :, :, k2 : k2 + 1],
                                               scalar=-SHAPES[ch // 3][k2], in1=gc_in[:, g, :, :, 2 + k2 : 3 + k2],
                                               op0=ALU.mult, op1=ALU.mult)

        def t1(ch, g):
            if not ok(ch):
                return
            dw = dns[ch][:].rearrange("p g j a f -> p (g j a f)").bitcast(F32)
            tp = tpp.tile([P, 2, 2, P], F32, name="tp")
            for u in range(2):
                for j in range(2):
                    sl = 2 * g + j
                    nc.tensor.transpose(tp[:, u, j, :], dw[:, 256 * sl + u : 256 * (sl + 1) : 2], perm[:])
            tps[(ch, g)] = tp

        def tp_out(ch, g, on_vector):
            if not ok(ch):
                return
            if g == 0:
                gg = work.tile([P, 4, P, 4], BF16, name="gg", align_bytes=64)
                ggs[ch] = gg
            gg = ggs[ch]
            ggw = gg[:].rearrange("p j r t -> p (j r t)").bitcast(F32).rearrange("p (j r u) -> p j r u", j=4, r=128, u=2)
            src = tps.pop((ch, g))[:].rearrange("p u j (b m) -> p (j b) m u", b=2)
            if on_vector:
                nc.vector.tensor_copy(out=ggw[:, :, 64 * g : 64 * g + 64, :], in_=src)
            else:
                nc.scalar.copy(out=ggw[:, :, 64 * g : 64 * g + 64, :], in_=src)

        def g_quant(ch):
            if not ok(ch):
                return
            gc = codes.tile([P, 512], U32, name="gc", align_bytes=64)
            gsc = codes.tile([P, 512], U8, name="gsc", align_bytes=64)
            nc.vector.quantize_mx(out=gc[:].bitcast(E5X4), scales=gsc[:], in_=ggs.pop(ch)[:].rearrange("p j r t -> p (j r t)"))
            gcs[ch] = (gc, gsc)

        def t_y(ch):
            if not ok(ch):
                return
            gw = ggs[ch][:].rearrange("p j r t -> p (j r t)").bitcast(F32)
            pair = []
            for u in range(2):
                ty = tpp.tile([P, 4, P], F32, name="tp")
                for j in range(4):
                    nc.tensor.transpose(ty[:, j, :], gw[:, 256 * j + u : 256 * (j + 1) : 2], ident[:])
                pair.append(ty)
            tys[ch] = pair

        def ty_out(ch, u, on_vector):
            if not ok(ch):
                return
            if u == 0:
                ai = work.tile([P, 2, 2, P, 4], BF16, name="ai", align_bytes=64)
                ais[ch] = ai
            ai = ais[ch]
            src = tys[ch][u][:].rearrange("m j p -> m (j p)").bitcast(BF16).rearrange("m (j p e) -> m e p j", j=4, p=128, e=2)
            if on_vector:
                nc.vector.tensor_copy(out=ai[:, u], in_=src)
            else:
                nc.scalar.copy(out=ai[:, u], in_=src)

        def a_quant(ch):
            if not ok(ch):
                return
            ac = codes.tile([P, 512], U32, name="ac", align_bytes=64)
            asc = codes.tile([P, 512], U8, name="asc", align_bytes=64)
            nc.vector.quantize_mx(out=ac[:].bitcast(E5X4), scales=asc[:], in_=ais.pop(ch)[:].rearrange("m u e p j -> m (u e p j)"))
            acs[ch] = (ac, asc)

        def mm1(ch, m):
            if not ok(ch):
                return
            ac, asc = acs[ch]
            o1 = o1p.tile([P, C], F32, name="o1")
            nc.tensor.matmul_mx(out=o1[:], lhsT=ac[:, 128 * m : 128 * m + 128].bitcast(E5X4),
                                lhsT_scale=asc[:, 128 * m : 128 * m + 128],
                                rhs=xc[:].bitcast(E4X4), rhs_scale=xs[:], start=True, stop=True)
            o1s[(ch, m)] = o1

        def evict(ch, m, on_vector):
            if not ok(ch):
                return
            if m % 2 == 0:
                st = stage.tile([P, 2, C], F32, name="st")
                sts[(ch, m // 2)] = st
            st = sts[(ch, m // 2)]
            o1 = o1s.pop((ch, m))
            if on_vector:
                nc.vector.tensor_scalar(out=st[:, m % 2, :], in0=o1[:], scalar1=-1.0, scalar2=None, op0=ALU.mult)
            else:
                nc.scalar.activation(out=st[:, m % 2, :], in_=o1[:], func=ACT.Copy, scale=-1.0)

        def store(ch, half, ring):
            if not ok(ch):
                return
            dst = out_1[512 * ch : 512 * ch + 512, :].rearrange("(p t) c -> p t c", t=4)
            ring.dma_start(out=dst[:, 2 * half : 2 * half + 2, :], in_=sts.pop((ch, half))[:])

        def mm0(ch):
            if not ok(ch):
                return
            wc, wsc = wcs.pop(ch)
            gc, gsc = gcs.pop(ch)
            for ct in range(4):
                nc.tensor.matmul_mx(out=acc[ct][:], lhsT=wc[:, 128 * ct : 128 * ct + 128].bitcast(E4X4),
                                    lhsT_scale=wsc[:, 128 * ct : 128 * ct + 128],
                                    rhs=gc[:].bitcast(E5X4), rhs_scale=gsc[:],
                                    start=(ch == 0), stop=(ch == NCH - 1))

        def evict0(ct, on_vector):
            o0 = stage0.tile([P, P, 2, 2], F32, name="o0")
            src = acc[ct][:].rearrange("c (j b m) -> c m b j", j=2, b=2)
            if on_vector:
                nc.vector.tensor_scalar(out=o0[:], in0=src, scalar1=-1.0, scalar2=None, op0=ALU.mult)
            else:
                nc.scalar.activation(out=o0[:], in_=src, func=ACT.Copy, scale=-1.0)
            nc.sync.dma_start(
                out=out_0[:, 128 * ct : 128 * ct + 128, :, :].rearrange("b c gy gx -> c b (gy gx)"),
                in_=o0[:].rearrange("c m b j -> c (m b j)").rearrange("c (i s) -> c i s", i=NB),
            )

        warm = const.tile([P, 1], F32, name="warm")
        nc.vector.memset(warm[:], 0.0)
        warm2 = const.tile([P, 1], F32, name="warm2")
        nc.scalar.activation(out=warm2[:], in_=warm[:], func=ACT.Exp)
        ident = const.tile([P, P], F32, name="ident")
        make_identity(nc, ident[:])
        perm = const.tile([P, P], F32, name="perm")
        nc.vector.tensor_copy(out=perm[:].rearrange("p (b m) -> p b m", b=2), in_=ident[:].rearrange("p (m b) -> p b m", b=2))
        acc = [accp.tile([P, 512], F32, name="acc%d" % ct) for ct in range(4)]

        xraw = const.tile([P, NB, 4, 64], BF16, name="xraw")
        nc.sync.dma_start(out=xraw[:], in_=x0.rearrange("b (q cl) gy gx -> q b cl (gy gx)", cl=4))
        for g in range(2):
            load_part(0, g, 0)
            load_part(0, g, 1)
        load_group(1, 0)
        load_group(1, 1)
        load_w(0)
        load_group(2, 0)
        load_w(1)
        load_group(2, 1)
        xr = const.tile([P, 4, 512], BF16, name="xr")
        xg = const.tile([P, C, 4], BF16, name="xg", align_bytes=64)
        xc = const.tile([P, C], U32, name="xc", align_bytes=64)
        xs = const.tile([P, C], U8, name="xs", align_bytes=64)

        act_e(0, True)

        nc.vector.tensor_copy(out=xr[:].rearrange("q cl (b s) -> q cl b s", b=NB), in_=xraw[:].rearrange("q b cl s -> q cl b s"))
        xw = xr[:].rearrange("q cl t -> q (cl t)").bitcast(F32)
        xgv = xg[:].rearrange("p (q cl) t -> p cl q t", cl=4)
        for h in range(2):
            xt = o1p.tile([P, 2, 2, P], F32, name="o1")
            for k2 in range(2):
                cl = 2 * h + k2
                for u in range(2):
                    nc.tensor.transpose(xt[:, k2, u, :], xw[:, 256 * cl + u : 256 * (cl + 1) : 2], ident[:])
            for k2 in range(2):
                cl = 2 * h + k2
                src = xt[:, k2].rearrange("p u q -> p (u q)").bitcast(BF16).rearrange("p (u q e) -> p q e u", u=2, q=128, e=2)
                nc.vector.tensor_copy(out=xgv[:, cl].rearrange("p q (e u) -> p q e u", e=2), in_=src)
        nc.vector.quantize_mx(out=xc[:].bitcast(E4X4), scales=xs[:], in_=xg[:].rearrange("p c t -> p (c t)"))

        for k in range(0, NCH + 3):
            if k == 1:
                load_group(3, 0)
                load_group(3, 1)
            if k == 3:
                load_group(4, 1)
                load_group(4, 0)
            if k == 5:
                load_group(5, 0)
            load_w(k + 2)
            late = k >= NCH - 1
            ring = nc.sync if late else nc.gpsimd
            tail = k >= NCH
            ty_out(k - 1, 0, False)
            ty_out(k - 1, 1, tail)
            evict(k - 2, 0, False)
            evict(k - 2, 1, False)
            store(k - 2, 0, ring)
            act_e(k + 1, k + 1 == NCH - 1)
            if k == 0 or k == NCH - 1:
                p3_half(k, 0)
                spec(k, 0)
                t1(k, 0)
                p3_half(k, 1)
                g_quant(k - 1)
                spec(k, 1)
                t1(k, 1)
            else:
                p3(k)
                g_quant(k - 1)
                spec(k, 0)
                spec(k, 1)
                t1(k, 0)
                t1(k, 1)
            w_int(k - 1)
            mm1(k - 2, 2)
            mm1(k - 2, 3)
            tp_out(k, 0, k != NCH - 1)
            tp_out(k, 1, True)
            t_y(k)
            a_quant(k - 1)
            w_quant(k - 1)
            mm0(k - 1)
            if k == NCH:
                evict0(0, False)
                evict0(1, True)
            evict(k - 2, 2, True)
            evict(k - 2, 3, True)
            store(k - 2, 1, ring)
            mm1(k - 1, 0)
            mm1(k - 1, 1)
            if k == NCH:
                evict0(2, False)
                evict0(3, True)
